import numpy as np
import ml_dtypes


def mxq(x, axis, fmt="e4m3"):
    dtype, down = {"e4m3": (ml_dtypes.float8_e4m3fn, 7), "e5m2": (ml_dtypes.float8_e5m2, 14)}[fmt]
    v = np.moveaxis(np.asarray(x, np.float32).astype(ml_dtypes.bfloat16).astype(np.float64), axis, -1)
    blocks = v.reshape(v.shape[:-1] + (-1, 32))
    amax = np.abs(blocks).max(-1, keepdims=True)
    byte = np.maximum(np.where(amax > 0, np.frexp(amax)[1] - 1 + 127, 0) - down, 1)
    scale = np.exp2(byte - 127.0)
    codes = (blocks / scale).astype(np.float32).astype(dtype).astype(np.float64)
    return np.moveaxis((codes * scale).reshape(v.shape), -1, axis)


WIDE = False


def mx_kscale(k):
    if not WIDE:
        return np.ones(k)
    levels = np.array([10, -10, 5, -5, 0])
    if k % 512:
        return np.exp2(np.random.permutation(np.resize(levels, k // 32))).repeat(32)
    a = np.empty((k // 512, 16))
    for p in range(k // 512):
        a[p, :8] = np.random.permutation(np.resize(levels, 8))
        for g in range(8):
            far = levels[np.abs(levels - a[p, g]) >= 10]
            a[p, g + 8] = far[np.random.randint(len(far))]
    return np.exp2(a.ravel()).repeat(32)


BF16 = ml_dtypes.bfloat16


def bf(x):
    return np.asarray(x, np.float32).astype(BF16)


def f64(x):
    return np.asarray(x).astype(np.float64)


B, C, P, NH, G, HH, WW = 4, 2048, 512, 32, 16, 16, 32
N = HH * WW
EPS = 1e-5


def group_norm(x, gamma, beta):
    xg = x.reshape(B, G, (C // G) * N)
    mean = xg.mean(axis=-1, keepdims=True)
    var = xg.var(axis=-1, keepdims=True)
    xn = ((xg - mean) / np.sqrt(var + EPS)).reshape(B, C, N)
    return xn * gamma[None, :, None] + beta[None, :, None]


def setup_inputs():
    s = mx_kscale(P)
    return {
        "feat": bf(np.random.standard_normal((B, C, HH, WW))),
        "h_attn": bf(np.random.standard_normal((B, P, HH, WW)) * 0.5 * s[None, :, None, None]),
        "w_out": bf(np.random.standard_normal((C, P)) * 2.0 / np.sqrt(P) / s[None, :]),
        "b_out": bf(np.random.standard_normal(C) * 0.3),
        "gamma": bf(1.0 + 0.1 * np.random.standard_normal(C)),
        "beta": bf(0.1 * np.random.standard_normal(C)),
    }


def reference(feat, h_attn, w_out, b_out, gamma, beta):
    y = (mxq(f64(w_out), 1, "e4m3") @ mxq(f64(h_attn).reshape(B, P, N), 1, "e4m3")) + f64(b_out)[None, :, None]
    x = f64(feat).reshape(B, C, N) + y
    return group_norm(x, f64(gamma), f64(beta)).reshape(B, C, HH, WW)

@@ -1,0 +1,319 @@
+from contextlib import ExitStack
+
+import concourse.mybir as mybir
+from concourse.masks import make_identity
+
+F32 = mybir.dt.float32
+BF16 = mybir.dt.bfloat16
+U32 = mybir.dt.uint32
+U8 = mybir.dt.uint8
+FP8X4 = mybir.dt.float8_e4m3fn_x4
+ALU = mybir.AluOpType
+ACT = mybir.ActivationFunctionType
+AX = mybir.AxisListType
+
+P = 128
+PACK = 4
+BATCH = 4
+CHANNELS = 2048
+K = 512
+N = 512
+GROUP = 128
+EPS = 1e-5
+
+ROWS = 4
+SLAB = P * ROWS
+SLABS = CHANNELS // SLAB
+TOTAL = BATCH * SLABS
+QUADRANT = GROUP // ROWS
+
+FLOPS = 2 * BATCH * CHANNELS * K * N
+
+HALF = ROWS // 2
+ROWS_ON_SCALAR = 1
+LAG = 2
+AHEAD = 16
+
+
+def tile_crossattention_pa_kernel(tc, feat, h_attn, w_out, b_out, gamma, beta, out):
+    nc = tc.nc
+
+    feat_v = feat.rearrange("b (s p j) h w -> (b s) p j (h w)", p=P, j=ROWS)
+    out_v = out.rearrange("b (s p j) h w -> (b s) p j (h w)", p=P, j=ROWS)
+    w_v = w_out.rearrange("(s p j) k -> s p j k", p=P, j=ROWS)
+    h_v = h_attn.rearrange("b (q t) h w -> b q t (h w)", t=PACK)
+
+    with ExitStack() as ctx:
+        const = ctx.enter_context(tc.tile_pool(name="const", bufs=1))
+        raw = ctx.enter_context(tc.tile_pool(name="raw", bufs=4))
+        grouped = ctx.enter_context(tc.tile_pool(name="grouped", bufs=2))
+        feats = ctx.enter_context(tc.tile_pool(name="feats", bufs=16))
+        xs = ctx.enter_context(tc.tile_pool(name="xs", bufs=9))
+        junk = ctx.enter_context(tc.tile_pool(name="junk", bufs=3))
+        small = ctx.enter_context(tc.tile_pool(name="small", bufs=4))
+        psum_y = ctx.enter_context(tc.psum_pool(name="psum_y", bufs=4))
+        psum_const = ctx.enter_context(tc.psum_pool(name="psum_const", bufs=1))
+        psum_t = ctx.enter_context(tc.psum_pool(name="psum_t", bufs=2))
+        psum_s = ctx.enter_context(tc.psum_pool(name="psum_s", bufs=1))
+
+        eps = const.tile([P, 1], F32)
+        nc.vector.memset(eps[:], EPS)
+        warm = const.tile([P, 1], F32)
+        nc.scalar.activation(out=warm[:], in_=eps[:], func=ACT.Abs_reciprocal_sqrt)
+
+        ident = const.tile([P, P], F32)
+        make_identity(nc, ident[:])
+
+        group_avg = const.tile([P, P], F32)
+        nc.vector.memset(group_avg[:], 0.0)
+        for g in range(P // QUADRANT):
+            rows = slice(g * QUADRANT, (g + 1) * QUADRANT)
+            nc.vector.memset(group_avg[rows, rows], -1.0 / (GROUP * N))
+
+        params_bf = const.tile([P, 3, SLABS, ROWS], BF16)
+        for which, vec in enumerate((b_out, gamma, beta)):
+            nc.scalar.dma_start(
+                out=params_bf[:, which], in_=vec.rearrange("(s p j) -> p s j", p=P, j=ROWS)
+            )
+        params = const.tile([P, 3, SLABS, ROWS], F32)
+
+        w_codes = const.tile([P, SLABS, SLAB], U32, align_bytes=64)
+        w_scales = const.tile([P, SLABS, SLAB], U8, align_bytes=64)
+        h_codes = const.tile([P, BATCH, N], U32, align_bytes=64)
+        h_scales = const.tile([P, BATCH, N], U8, align_bytes=64)
+
+        h_raw = {}
+        w_raw = {}
+        h_grouped = {}
+        w_grouped = {}
+        feat_sb = {}
+        y_ps = {}
+        x_sb = {}
+        sums_sb = {}
+        mom_ps = {}
+        neg_mean_sb = {}
+        neg_var_sb = {}
+        rstd_sb = {}
+        gain_sb = {}
+        shift_sb = {}
+
+        def load_operands(i):
+            b, s = divmod(i, SLABS)
+            if i < TOTAL and b == 0:
+                w_tile = raw.tile([P, ROWS, K], BF16)
+                nc.sync.dma_start(out=w_tile[:], in_=w_v[s])
+                w_raw[s] = w_tile
+            if i < TOTAL and s == 0:
+                h_tile = raw.tile([P, PACK, N], BF16)
+                nc.sync.dma_start(out=h_tile[:], in_=h_v[b])
+                h_raw[b] = h_tile
+
+        def load_feat(i):
+            if i < TOTAL:
+                feat_tile = feats.tile([P, ROWS, N], BF16)
+                nc.sync.dma_start(out=feat_tile[:], in_=feat_v[i])
+                feat_sb[i] = feat_tile
+
+        def regroup(i):
+            b, s = divmod(i, SLABS)
+            if b == 0:
+                w_words = w_raw[s][:].rearrange("p j k -> p (j k)").bitcast(F32)
+                w_group = grouped.tile([P, ROWS * P * PACK], BF16, align_bytes=64)
+                w_group_words = w_group[:].bitcast(F32).rearrange("q (j p u) -> q j p u", j=ROWS, u=2)
+                for half in range(2):
+                    w_t = psum_t.tile([P, 2, 2, P], F32)
+                    for jj in range(2):
+                        for u in range(2):
+                            row = (2 * half + jj) * 2 * P
+                            nc.tensor.transpose(w_t[:, jj, u, :], w_words[:, row + u : row + 2 * P : 2], ident[:])
+                    nc.scalar.copy(
+                        out=w_group_words[:, 2 * half : 2 * half + 2],
+                        in_=w_t[:].rearrange("q jj u p -> q jj p u"),
+                    )
+                w_grouped[s] = w_group
+            if s == 0:
+                h_group = grouped.tile([P, N, PACK], BF16, align_bytes=64)
+                nc.vector.tensor_copy(
+                    out=h_group[:].rearrange("q (c i) t -> q c t i", i=4),
+                    in_=h_raw[b][:].rearrange("q t (c i) -> q c t i", i=4),
+                )
+                h_grouped[b] = h_group
+
+        def quantise(i):
+            b, s = divmod(i, SLABS)
+            if b == 0:
+                nc.vector.quantize_mx(
+                    out=w_codes[:, s, :].bitcast(FP8X4), scales=w_scales[:, s, :], in_=w_grouped[s][:]
+                )
+            if s == 0:
+                nc.vector.quantize_mx(
+                    out=h_codes[:, b, :].bitcast(FP8X4),
+                    scales=h_scales[:, b, :],
+                    in_=h_grouped[b][:].rearrange("q n t -> q (n t)"),
+                )
+
+        def project(i, j):
+            b, s = divmod(i, SLABS)
+            y = psum_y.tile([P, N], F32)
+            cols = slice(j * P, (j + 1) * P)
+            nc.tensor.matmul_mx(
+                out=y[:],
+                lhsT=w_codes[:, s, cols].bitcast(FP8X4),
+                lhsT_scale=w_scales[:, s, cols],
+                rhs=h_codes[:, b, :].bitcast(FP8X4),
+                rhs_scale=h_scales[:, b, :],
+                start=True,
+                stop=True,
+            )
+            y_ps[(i, j)] = y
+
+        def residual(i, j):
+            s = i % SLABS
+            half, r = divmod(j, HALF)
+            if j == 0:
+                x = xs.tile([P, ROWS, N], F32)
+                x_sb[i] = x
+                sums = small.tile([P, 2, HALF + 1, 8], F32)
+                sums_sb[i] = sums
+            nc.vector.scalar_tensor_tensor(
+                out=x_sb[i][:, j, :],
+                in0=y_ps[(i, j)][:],
+                scalar=params[:, 0, s, j : j + 1],
+                in1=feat_sb[i][:, j, :],
+                op0=ALU.add,
+                op1=ALU.add,
+                accum_out=sums_sb[i][:, half, r, 0:1],
+            )
+
+        def squares(i, half):
+            sq = junk.tile([P, HALF * N], BF16)
+            nc.scalar.activation(
+                out=sq[:],
+                in_=x_sb[i][:, half * HALF : (half + 1) * HALF, :].rearrange("p j n -> p (j n)"),
+                func=ACT.Square,
+                accum_out=sums_sb[i][:, half, HALF, 0:1],
+            )
+            if half == 0:
+                mom = psum_s.tile([P, HALF + 1], F32)
+                mom_ps[i] = mom
+            nc.tensor.matmul(
+                out=mom_ps[i][:],
+                lhsT=group_avg[:],
+                rhs=sums_sb[i][:, half, :, 0],
+                start=(half == 0),
+                stop=(half == 1),
+            )
+
+        def mean(i):
+            neg_mean = small.tile([P, 1], F32)
+            nc.vector.tensor_reduce(out=neg_mean[:], in_=mom_ps[i][:, 0:HALF], axis=AX.X, op=ALU.add)
+            neg_mean_sb[i] = neg_mean
+
+        def variance(i):
+            neg_var = small.tile([P, 1], F32)
+            nc.vector.scalar_tensor_tensor(
+                out=neg_var[:],
+                in0=neg_mean_sb[i][:],
+                scalar=neg_mean_sb[i][:, 0:1],
+                in1=mom_ps[i][:, HALF : HALF + 1],
+                op0=ALU.mult,
+                op1=ALU.add,
+            )
+            neg_var_sb[i] = neg_var
+
+        def inv_std(i):
+            rstd = small.tile([P, 1], F32)
+            nc.scalar.activation(
+                out=rstd[:], in_=neg_var_sb[i][:], func=ACT.Abs_reciprocal_sqrt, bias=eps[:, 0:1], scale=-1.0
+            )
+            rstd_sb[i] = rstd
+
+        def make_gain(i):
+            s = i % SLABS
+            gain = small.tile([P, ROWS], F32)
+            nc.vector.tensor_scalar(
+                out=gain[:], in0=affine_ps[:, 0, s, :], scalar1=rstd_sb[i][:, 0:1], scalar2=None, op0=ALU.mult
+            )
+            gain_sb[i] = gain
+
+        def make_shift(i):
+            s = i % SLABS
+            shift = small.tile([P, ROWS], F32)
+            nc.vector.scalar_tensor_tensor(
+                out=shift[:],
+                in0=gain_sb[i][:],
+                scalar=neg_mean_sb[i][:, 0:1],
+                in1=affine_ps[:, 1, s, :],
+                op0=ALU.mult,
+                op1=ALU.add,
+            )
+            shift_sb[i] = shift
+
+        def normalise(i):
+            x = x_sb[i]
+            helper = nc.vector if i >= TOTAL - LAG else nc.gpsimd
+            for j in range(ROWS):
+                gain_j = gain_sb[i][:, j : j + 1]
+                shift_j = shift_sb[i][:, j : j + 1]
+                if j < ROWS_ON_SCALAR:
+                    nc.scalar.activation(out=x[:, j, :], in_=x[:, j, :], func=ACT.Identity, bias=shift_j, scale=gain_j)
+                else:
+                    helper.tensor_scalar(
+                        out=x[:, j, :], in0=x[:, j, :], scalar1=gain_j, scalar2=shift_j, op0=ALU.mult, op1=ALU.add
+                    )
+            for half in range(2):
+                rows = slice(half * HALF, (half + 1) * HALF)
+                nc.sync.dma_start(out=out_v[i][:, rows, :], in_=x[:, rows, :])
+
+        ctx.enter_context(tc.manual_schedule())
+
+        load_operands(0)
+        load_operands(1)
+        for i in range(AHEAD):
+            load_feat(i)
+            load_operands(i + 2)
+
+        regroup(0)
+        regroup(1)
+        quantise(0)
+        nc.vector.tensor_copy(out=params[:], in_=params_bf[:])
+        for j in range(ROWS):
+            project(0, j)
+        affine_ps = psum_const.tile([P, 2, SLABS, ROWS], F32)
+        nc.tensor.matmul(
+            out=affine_ps[:].rearrange("p a s j -> p (a s j)"),
+            lhsT=ident[:],
+            rhs=params[:, 1:3].rearrange("p a s j -> p (a s j)"),
+            start=True,
+            stop=True,
+        )
+
+        for step in range(TOTAL + LAG):
+            here = step < TOTAL
+            after = step + 1 < TOTAL
+            stats = 1 <= step <= TOTAL
+            finish = step >= LAG
+            if after:
+                quantise(step + 1)
+            if step + 2 < TOTAL:
+                regroup(step + 2)
+            for j in range(ROWS):
+                if here:
+                    residual(step, j)
+                if after:
+                    project(step + 1, j)
+                if j == ROWS - 2 and stats:
+                    mean(step - 1)
+                if j == ROWS - 2 and finish:
+                    make_gain(step - LAG)
+                if j == ROWS - 1 and stats:
+                    variance(step - 1)
+                if j == ROWS - 1 and finish:
+                    make_shift(step - LAG)
+            for half in range(2):
+                if here:
+                    squares(step, half)
+            if stats:
+                inv_std(step - 1)
+            if finish:
+                normalise(step - LAG)

@@ -22,17 +22,16 @@ GROUP = 128
 EPS = 1e-5
 
 ROWS = 4
+HALF = ROWS // 2
 SLAB = P * ROWS
 SLABS = CHANNELS // SLAB
 TOTAL = BATCH * SLABS
+LAST = TOTAL - 1
 QUADRANT = GROUP // ROWS
 
 FLOPS = 2 * BATCH * CHANNELS * K * N
 
-HALF = ROWS // 2
 ROWS_ON_SCALAR = 1
-LAG = 2
-AHEAD = 16
 
 
 def tile_crossattention_pa_kernel(tc, feat, h_attn, w_out, b_out, gamma, beta, out):
@@ -51,10 +50,9 @@ def tile_crossattention_pa_kernel(tc, feat, h_attn, w_out, b_out, gamma, beta, o
         xs = ctx.enter_context(tc.tile_pool(name="xs", bufs=9))
         junk = ctx.enter_context(tc.tile_pool(name="junk", bufs=3))
         small = ctx.enter_context(tc.tile_pool(name="small", bufs=4))
-        psum_y = ctx.enter_context(tc.psum_pool(name="psum_y", bufs=4))
+        psum_y = ctx.enter_context(tc.psum_pool(name="psum_y", bufs=5))
         psum_const = ctx.enter_context(tc.psum_pool(name="psum_const", bufs=1))
-        psum_t = ctx.enter_context(tc.psum_pool(name="psum_t", bufs=2))
-        psum_s = ctx.enter_context(tc.psum_pool(name="psum_s", bufs=1))
+        psum_s = ctx.enter_context(tc.psum_pool(name="psum_s", bufs=2))
 
         eps = const.tile([P, 1], F32)
         nc.vector.memset(eps[:], EPS)
@@ -63,6 +61,8 @@ def tile_crossattention_pa_kernel(tc, feat, h_attn, w_out, b_out, gamma, beta, o
 
         ident = const.tile([P, P], F32)
         make_identity(nc, ident[:])
+        ident_bf = const.tile([P, P], BF16)
+        nc.gpsimd.tensor_copy(out=ident_bf[:], in_=ident[:])
 
         group_avg = const.tile([P, P], F32)
         nc.vector.memset(group_avg[:], 0.0)
@@ -85,7 +85,9 @@ def tile_crossattention_pa_kernel(tc, feat, h_attn, w_out, b_out, gamma, beta, o
         h_raw = {}
         w_raw = {}
         h_grouped = {}
+        h_spread = {}
         w_grouped = {}
+        w_transposed = {}
         feat_sb = {}
         y_ps = {}
         x_sb = {}
@@ -97,67 +99,111 @@ def tile_crossattention_pa_kernel(tc, feat, h_attn, w_out, b_out, gamma, beta, o
         gain_sb = {}
         shift_sb = {}
 
-        def load_operands(i):
-            b, s = divmod(i, SLABS)
-            if i < TOTAL and b == 0:
+        order = []
+        for b in range(BATCH):
+            order.extend([(b, s) for s in range(SLABS)])
+
+        def new_h(i):
+            if i < TOTAL and order[i][1] == 0:
+                return order[i][0]
+            return None
+
+        def new_w(i):
+            if i < TOTAL and order[i][0] == 0:
+                return order[i][1]
+            return None
+
+        def half_rows(half):
+            return slice(half * HALF, (half + 1) * HALF)
+
+        def load_w(s, halves):
+            if s not in w_raw:
                 w_tile = raw.tile([P, ROWS, K], BF16)
-                nc.sync.dma_start(out=w_tile[:], in_=w_v[s])
                 w_raw[s] = w_tile
-            if i < TOTAL and s == 0:
-                h_tile = raw.tile([P, PACK, N], BF16)
-                nc.sync.dma_start(out=h_tile[:], in_=h_v[b])
-                h_raw[b] = h_tile
+            for rows in halves:
+                nc.sync.dma_start(out=w_raw[s][:, rows, :], in_=w_v[s][:, rows, :])
 
-        def load_feat(i):
-            if i < TOTAL:
+        def load_h(b, pieces):
+            h_tile = raw.tile([P, PACK, N], BF16)
+            for values in pieces:
+                nc.sync.dma_start(out=h_tile[:, values, :], in_=h_v[b][:, values, :])
+            h_raw[b] = h_tile
+
+        def load_feat(i, pieces):
+            if i not in feat_sb:
                 feat_tile = feats.tile([P, ROWS, N], BF16)
-                nc.sync.dma_start(out=feat_tile[:], in_=feat_v[i])
                 feat_sb[i] = feat_tile
+            for rows in pieces:
+                nc.sync.dma_start(out=feat_sb[i][:, rows, :], in_=feat_v[order[i][0] * SLABS + order[i][1]][:, rows, :])
 
-        def regroup(i):
-            b, s = divmod(i, SLABS)
-            if b == 0:
-                w_words = w_raw[s][:].rearrange("p j k -> p (j k)").bitcast(F32)
-                w_group = grouped.tile([P, ROWS * P * PACK], BF16, align_bytes=64)
-                w_group_words = w_group[:].bitcast(F32).rearrange("q (j p u) -> q j p u", j=ROWS, u=2)
-                for half in range(2):
-                    w_t = psum_t.tile([P, 2, 2, P], F32)
-                    for jj in range(2):
-                        for u in range(2):
-                            row = (2 * half + jj) * 2 * P
-                            nc.tensor.transpose(w_t[:, jj, u, :], w_words[:, row + u : row + 2 * P : 2], ident[:])
-                    nc.scalar.copy(
-                        out=w_group_words[:, 2 * half : 2 * half + 2],
-                        in_=w_t[:].rearrange("q jj u p -> q jj p u"),
-                    )
-                w_grouped[s] = w_group
-            if s == 0:
+        def transpose_w(s):
+            w_words = w_raw[s][:].rearrange("p j k -> p (j k)").bitcast(F32)
+            for half in range(2):
+                bank = psum_y.tile([P, N], F32)
+                w_t = bank[:].rearrange("q (jj u p) -> q jj u p", jj=HALF, u=2)
+                for jj in range(HALF):
+                    for u in range(2):
+                        row = (HALF * half + jj) * 2 * P
+                        nc.tensor.transpose(w_t[:, jj, u, :], w_words[:, row + u : row + 2 * P : 2], ident[:])
+                w_transposed[(s, half)] = w_t
+
+        def regroup_w(s):
+            w_group = grouped.tile([P, ROWS * P * PACK], BF16, align_bytes=64)
+            w_group_words = w_group[:].bitcast(F32).rearrange("q (j p u) -> q j p u", j=ROWS, u=2)
+            for half in range(2):
+                nc.scalar.copy(
+                    out=w_group_words[:, half_rows(half)],
+                    in_=w_transposed[(s, half)].rearrange("q jj u p -> q jj p u"),
+                )
+            w_grouped[s] = w_group
+
+        def regroup_h(b):
+            h_group = grouped.tile([P, N, PACK], BF16, align_bytes=64)
+            dst = h_group[:].rearrange("q (c i) t -> q c t i", i=4)
+            src = h_raw[b][:].rearrange("q t (c i) -> q c t i", i=4)
+            nc.vector.tensor_copy(out=dst, in_=src)
+            h_grouped[b] = h_group
+
+        def spread_h(b, half):
+            bank = psum_y.tile([P, N // 2, PACK], BF16)
+            for part in range(2):
+                first = (2 * half + part) * P
+                nc.tensor.matmul(
+                    out=bank[:, part * P : (part + 1) * P, :],
+                    lhsT=ident_bf[:],
+                    rhs=h_raw[b][:, :, first : first + P].rearrange("q t n -> q n t"),
+                    start=True,
+                    stop=True,
+                )
+            h_spread[(b, half)] = bank
+
+        def gather_h(b, half):
+            cols = slice(half * N // 2, (half + 1) * N // 2)
+            if half == 0:
                 h_group = grouped.tile([P, N, PACK], BF16, align_bytes=64)
-                nc.vector.tensor_copy(
-                    out=h_group[:].rearrange("q (c i) t -> q c t i", i=4),
-                    in_=h_raw[b][:].rearrange("q t (c i) -> q c t i", i=4),
-                )
                 h_grouped[b] = h_group
+            nc.scalar.copy(out=h_grouped[b][:, cols, :], in_=h_spread[(b, half)][:])
 
-        def quantise(i):
-            b, s = divmod(i, SLABS)
-            if b == 0:
-                nc.vector.quantize_mx(
-                    out=w_codes[:, s, :].bitcast(FP8X4), scales=w_scales[:, s, :], in_=w_grouped[s][:]
-                )
-            if s == 0:
-                nc.vector.quantize_mx(
-                    out=h_codes[:, b, :].bitcast(FP8X4),
-                    scales=h_scales[:, b, :],
-                    in_=h_grouped[b][:].rearrange("q n t -> q (n t)"),
-                )
+        def quantise_w(s, cols):
+            nc.vector.quantize_mx(
+                out=w_codes[:, s, cols].bitcast(FP8X4),
+                scales=w_scales[:, s, cols],
+                in_=w_grouped[s][:, cols.start * PACK : cols.stop * PACK],
+            )
+
+        def quantise_h(b):
+            nc.vector.quantize_mx(
+                out=h_codes[:, b, :].bitcast(FP8X4),
+                scales=h_scales[:, b, :],
+                in_=h_grouped[b][:].rearrange("q n t -> q (n t)"),
+            )
 
         def project(i, j):
-            b, s = divmod(i, SLABS)
-            y = psum_y.tile([P, N], F32)
+            b, s = order[i]
+            bank = psum_y.tile([P, N], F32)
             cols = slice(j * P, (j + 1) * P)
             nc.tensor.matmul_mx(
-                out=y[:],
+                out=bank[:],
                 lhsT=w_codes[:, s, cols].bitcast(FP8X4),
                 lhsT_scale=w_scales[:, s, cols],
                 rhs=h_codes[:, b, :].bitcast(FP8X4),
@@ -165,15 +211,18 @@ def tile_crossattention_pa_kernel(tc, feat, h_attn, w_out, b_out, gamma, beta, o
                 start=True,
                 stop=True,
             )
-            y_ps[(i, j)] = y
+            y_ps[(i, j)] = bank
+
+        def piece_rows(i):
+            return 1 if i == LAST else HALF
 
         def residual(i, j):
-            s = i % SLABS
-            half, r = divmod(j, HALF)
+            b, s = order[i]
+            n_rows = piece_rows(i)
             if j == 0:
                 x = xs.tile([P, ROWS, N], F32)
                 x_sb[i] = x
-                sums = small.tile([P, 2, HALF + 1, 8], F32)
+                sums = small.tile([P, ROWS // n_rows, n_rows + 1, 8], F32)
                 sums_sb[i] = sums
             nc.vector.scalar_tensor_tensor(
                 out=x_sb[i][:, j, :],
@@ -182,40 +231,45 @@ def tile_crossattention_pa_kernel(tc, feat, h_attn, w_out, b_out, gamma, beta, o
                 in1=feat_sb[i][:, j, :],
                 op0=ALU.add,
                 op1=ALU.add,
-                accum_out=sums_sb[i][:, half, r, 0:1],
+                accum_out=sums_sb[i][:, j // n_rows, j % n_rows, 0:1],
             )
 
-        def squares(i, half):
+        def squares(i, piece):
+            n_rows = piece_rows(i)
             sq = junk.tile([P, HALF * N], BF16)
             nc.scalar.activation(
-                out=sq[:],
-                in_=x_sb[i][:, half * HALF : (half + 1) * HALF, :].rearrange("p j n -> p (j n)"),
+                out=sq[:, : n_rows * N],
+                in_=x_sb[i][:, piece * n_rows : (piece + 1) * n_rows, :].rearrange("p j n -> p (j n)"),
                 func=ACT.Square,
-                accum_out=sums_sb[i][:, half, HALF, 0:1],
+                accum_out=sums_sb[i][:, piece, n_rows, 0:1],
             )
-            if half == 0:
+
+        def moments(i, piece):
+            n_rows = piece_rows(i)
+            if piece == 0:
                 mom = psum_s.tile([P, HALF + 1], F32)
                 mom_ps[i] = mom
             nc.tensor.matmul(
-                out=mom_ps[i][:],
+                out=mom_ps[i][:, : n_rows + 1],
                 lhsT=group_avg[:],
-                rhs=sums_sb[i][:, half, :, 0],
-                start=(half == 0),
-                stop=(half == 1),
+                rhs=sums_sb[i][:, piece, :, 0],
+                start=(piece == 0),
+                stop=(piece == ROWS // n_rows - 1),
             )
 
         def mean(i):
             neg_mean = small.tile([P, 1], F32)
-            nc.vector.tensor_reduce(out=neg_mean[:], in_=mom_ps[i][:, 0:HALF], axis=AX.X, op=ALU.add)
+            nc.vector.tensor_reduce(out=neg_mean[:], in_=mom_ps[i][:, : piece_rows(i)], axis=AX.X, op=ALU.add)
             neg_mean_sb[i] = neg_mean
 
         def variance(i):
             neg_var = small.tile([P, 1], F32)
+            n_rows = piece_rows(i)
             nc.vector.scalar_tensor_tensor(
                 out=neg_var[:],
                 in0=neg_mean_sb[i][:],
                 scalar=neg_mean_sb[i][:, 0:1],
-                in1=mom_ps[i][:, HALF : HALF + 1],
+                in1=mom_ps[i][:, n_rows : n_rows + 1],
                 op0=ALU.mult,
                 op1=ALU.add,
             )
@@ -229,7 +283,7 @@ def tile_crossattention_pa_kernel(tc, feat, h_attn, w_out, b_out, gamma, beta, o
             rstd_sb[i] = rstd
 
         def make_gain(i):
-            s = i % SLABS
+            b, s = order[i]
             gain = small.tile([P, ROWS], F32)
             nc.vector.tensor_scalar(
                 out=gain[:], in0=affine_ps[:, 0, s, :], scalar1=rstd_sb[i][:, 0:1], scalar2=None, op0=ALU.mult
@@ -237,7 +291,7 @@ def tile_crossattention_pa_kernel(tc, feat, h_attn, w_out, b_out, gamma, beta, o
             gain_sb[i] = gain
 
         def make_shift(i):
-            s = i % SLABS
+            b, s = order[i]
             shift = small.tile([P, ROWS], F32)
             nc.vector.scalar_tensor_tensor(
                 out=shift[:],
@@ -249,33 +303,44 @@ def tile_crossattention_pa_kernel(tc, feat, h_attn, w_out, b_out, gamma, beta, o
             )
             shift_sb[i] = shift
 
-        def normalise(i):
-            x = x_sb[i]
-            helper = nc.vector if i >= TOTAL - LAG else nc.gpsimd
-            for j in range(ROWS):
-                gain_j = gain_sb[i][:, j : j + 1]
-                shift_j = shift_sb[i][:, j : j + 1]
-                if j < ROWS_ON_SCALAR:
-                    nc.scalar.activation(out=x[:, j, :], in_=x[:, j, :], func=ACT.Identity, bias=shift_j, scale=gain_j)
-                else:
-                    helper.tensor_scalar(
-                        out=x[:, j, :], in0=x[:, j, :], scalar1=gain_j, scalar2=shift_j, op0=ALU.mult, op1=ALU.add
-                    )
-            for half in range(2):
-                rows = slice(half * HALF, (half + 1) * HALF)
-                nc.sync.dma_start(out=out_v[i][:, rows, :], in_=x[:, rows, :])
+        def normalise(i, j, engine):
+            row = x_sb[i][:, j, :]
+            gain_j = gain_sb[i][:, j : j + 1]
+            shift_j = shift_sb[i][:, j : j + 1]
+            if engine is nc.scalar:
+                nc.scalar.activation(out=row, in_=row, func=ACT.Identity, bias=shift_j, scale=gain_j)
+            else:
+                engine.tensor_scalar(out=row, in0=row, scalar1=gain_j, scalar2=shift_j, op0=ALU.mult, op1=ALU.add)
+
+        def store(i, rows):
+            nc.sync.dma_start(out=out_v[order[i][0] * SLABS + order[i][1]][:, rows, :], in_=x_sb[i][:, rows, :])
 
         ctx.enter_context(tc.manual_schedule())
 
-        load_operands(0)
-        load_operands(1)
-        for i in range(AHEAD):
-            load_feat(i)
-            load_operands(i + 2)
-
-        regroup(0)
-        regroup(1)
-        quantise(0)
+        all_rows = slice(0, ROWS)
+        all_cols = slice(0, SLAB)
+        halves = (half_rows(0), half_rows(1))
+        ROWS_ALL = TOTAL * ROWS
+        off = lambda i: (4, 5, 7, 8)
+        plan = lambda i: "SVVV" if i >= TOTAL - 3 else "SGGG"
+        load_w(0, (all_rows,))
+        load_h(0, (all_rows,))
+        load_w(1, (all_rows,))
+        load_feat(0, (all_rows,))
+        for i in range(1, TOTAL):
+            if new_w(i + 1) is not None:
+                load_w(new_w(i + 1), (all_rows,))
+            if new_h(i + 2) is not None:
+                load_h(new_h(i + 2), (all_rows,))
+            load_feat(i, (all_rows,))
+        regroup_h(0)
+        transpose_w(0)
+        regroup_w(0)
+        transpose_w(1)
+        regroup_w(1)
+        quantise_w(0, slice(0, SLAB // 2))
+        quantise_h(0)
+        quantise_w(0, slice(SLAB // 2, SLAB))
         nc.vector.tensor_copy(out=params[:], in_=params_bf[:])
         for j in range(ROWS):
             project(0, j)
@@ -288,32 +353,67 @@ def tile_crossattention_pa_kernel(tc, feat, h_attn, w_out, b_out, gamma, beta, o
             stop=True,
         )
 
-        for step in range(TOTAL + LAG):
-            here = step < TOTAL
-            after = step + 1 < TOTAL
-            stats = 1 <= step <= TOTAL
-            finish = step >= LAG
-            if after:
-                quantise(step + 1)
-            if step + 2 < TOTAL:
-                regroup(step + 2)
-            for j in range(ROWS):
-                if here:
-                    residual(step, j)
-                if after:
-                    project(step + 1, j)
-                if j == ROWS - 2 and stats:
-                    mean(step - 1)
-                if j == ROWS - 2 and finish:
-                    make_gain(step - LAG)
-                if j == ROWS - 1 and stats:
-                    variance(step - 1)
-                if j == ROWS - 1 and finish:
-                    make_shift(step - LAG)
-            for half in range(2):
-                if here:
-                    squares(step, half)
-            if stats:
-                inv_std(step - 1)
-            if finish:
-                normalise(step - LAG)
+        projected = set((0, j) for j in range(ROWS))
+        for t in range(ROWS_ALL + 12):
+            i, j = divmod(t, ROWS)
+            nxt = i + 1
+            if t < ROWS_ALL and j == 0 and False:
+                if new_w(nxt) is not None:
+                    quantise_w(new_w(nxt), all_cols)
+                if new_h(nxt) is not None:
+                    quantise_h(new_h(nxt))
+            if t < ROWS_ALL:
+                residual(i, j)
+            if t < ROWS_ALL and nxt < TOTAL:
+                fresh = new_w(nxt) is not None or new_h(nxt) is not None
+                if j == 9 and new_h(i + 1) is not None:
+                    regroup_h(new_h(i + 1))
+                if j == 1:
+                    if new_w(nxt) is not None:
+                        quantise_w(new_w(nxt), all_cols)
+                    if new_h(nxt) is not None:
+                        quantise_h(new_h(nxt))
+                for jj in range(j + 1):
+                    if (nxt, jj) not in projected and (not fresh or j >= 1):
+                        project(nxt, jj)
+                        projected.add((nxt, jj))
+            for b in range(1, BATCH):
+                first = [k for k in range(TOTAL) if new_h(k) == b][0]
+                for half in range(2):
+                    if t == ROWS * first - [11,9][half]:
+                        spread_h(b, half)
+            if t < ROWS_ALL and j == 0 and new_w(i + 2) is not None:
+                transpose_w(new_w(i + 2))
+            for k in range(TOTAL):
+                last = ROWS * k + ROWS - 1
+                m, v, g, h = off(k)
+                if t == last + m:
+                    mean(k)
+                if t == last + v:
+                    variance(k)
+                if t == last + g:
+                    make_gain(k)
+                if t == last + h:
+                    make_shift(k)
+            if t < ROWS_ALL:
+                n_rows = piece_rows(i)
+                if j % n_rows == n_rows - 1:
+                    squares(i, j // n_rows)
+                    if j == 1 and new_w(i + 2) is not None:
+                        regroup_w(new_w(i + 2))
+                    moments(i, j // n_rows)
+            for b in range(1, BATCH):
+                first = [k for k in range(TOTAL) if new_h(k) == b][0]
+                for half in range(2):
+                    if t == ROWS * first - [7,6][half]:
+                        gather_h(b, half)
+            for k in range(TOTAL):
+                if t == ROWS * k + ROWS - 1 + off(k)[1]:
+                    inv_std(k)
+            for k in range(TOTAL):
+                if t == ROWS * k + ROWS - 1 + off(k)[3]:
+                    p = plan(k)
+                    for r in range(ROWS):
+                        normalise(k, r, {"S": nc.scalar, "G": nc.gpsimd, "V": nc.vector}[p[r]])
+                    store(k, halves[0])
+                    store(k, halves[1])

@@ -31,6 +31,7 @@ QUADRANT = GROUP // ROWS
 
 FLOPS = 2 * BATCH * CHANNELS * K * N
 
+SINGLES = 4
 ROWS_ON_SCALAR = 1
 
 
@@ -46,7 +47,9 @@ def tile_crossattention_pa_kernel(tc, feat, h_attn, w_out, b_out, gamma, beta, o
         const = ctx.enter_context(tc.tile_pool(name="const", bufs=1))
         raw = ctx.enter_context(tc.tile_pool(name="raw", bufs=4))
         grouped = ctx.enter_context(tc.tile_pool(name="grouped", bufs=2))
-        feats = ctx.enter_context(tc.tile_pool(name="feats", bufs=16))
+        feats = ctx.enter_context(tc.tile_pool(name="feats", bufs=SINGLES))
+        feat_pairs = ctx.enter_context(tc.tile_pool(name="feat_pairs", bufs=(TOTAL - SINGLES) // 2))
+        h_pairs = ctx.enter_context(tc.tile_pool(name="h_pairs", bufs=1))
         xs = ctx.enter_context(tc.tile_pool(name="xs", bufs=9))
         junk = ctx.enter_context(tc.tile_pool(name="junk", bufs=3))
         small = ctx.enter_context(tc.tile_pool(name="small", bufs=4))
@@ -129,6 +132,18 @@ def tile_crossattention_pa_kernel(tc, feat, h_attn, w_out, b_out, gamma, beta, o
                 nc.sync.dma_start(out=h_tile[:, values, :], in_=h_v[b][:, values, :])
             h_raw[b] = h_tile
 
+        def load_feat_pair(i):
+            pair = feat_pairs.tile([P, 2, ROWS, N], BF16)
+            nc.sync.dma_start(out=pair[:], in_=feat_v[i : i + 2].rearrange("s p j n -> p s j n"))
+            feat_sb[i] = pair[:, 0]
+            feat_sb[i + 1] = pair[:, 1]
+
+        def load_h_pair(b):
+            pair = h_pairs.tile([P, 2, PACK, N], BF16)
+            nc.sync.dma_start(out=pair[:], in_=h_v[b : b + 2].rearrange("b q t n -> q b t n"))
+            h_raw[b] = pair[:, 0]
+            h_raw[b + 1] = pair[:, 1]
+
         def load_feat(i, pieces):
             if i not in feat_sb:
                 feat_tile = feats.tile([P, ROWS, N], BF16)
@@ -164,18 +179,18 @@ def tile_crossattention_pa_kernel(tc, feat, h_attn, w_out, b_out, gamma, beta, o
             nc.vector.tensor_copy(out=dst, in_=src)
             h_grouped[b] = h_group
 
-        def spread_h(b, half):
-            bank = psum_y.tile([P, N // 2, PACK], BF16)
-            for part in range(2):
-                first = (2 * half + part) * P
-                nc.tensor.matmul(
-                    out=bank[:, part * P : (part + 1) * P, :],
-                    lhsT=ident_bf[:],
-                    rhs=h_raw[b][:, :, first : first + P].rearrange("q t n -> q n t"),
-                    start=True,
-                    stop=True,
-                )
-            h_spread[(b, half)] = bank
+        def spread_h(b, part):
+            half, side = divmod(part, 2)
+            if side == 0:
+                bank = psum_y.tile([P, N // 2, PACK], BF16)
+                h_spread[(b, half)] = bank
+            nc.tensor.matmul(
+                out=h_spread[(b, half)][:, side * P : (side + 1) * P, :],
+                lhsT=ident_bf[:],
+                rhs=h_raw[b][:, :, part * P : (part + 1) * P].rearrange("q t n -> q n t"),
+                start=True,
+                stop=True,
+            )
 
         def gather_h(b, half):
             cols = slice(half * N // 2, (half + 1) * N // 2)
@@ -214,7 +229,7 @@ def tile_crossattention_pa_kernel(tc, feat, h_attn, w_out, b_out, gamma, beta, o
             y_ps[(i, j)] = bank
 
         def piece_rows(i):
-            return 1 if i == LAST else HALF
+            return 1 if i >= TOTAL - 0 else HALF
 
         def residual(i, j):
             b, s = order[i]
@@ -322,17 +337,21 @@ def tile_crossattention_pa_kernel(tc, feat, h_attn, w_out, b_out, gamma, beta, o
         halves = (half_rows(0), half_rows(1))
         ROWS_ALL = TOTAL * ROWS
         off = lambda i: (4, 5, 7, 8)
-        plan = lambda i: "SVVV" if i >= TOTAL - 3 else "SGGG"
+        plan = lambda i: {TOTAL - 3: "SVGG", TOTAL - 2: "SSVV", TOTAL - 1: "SSVV"}.get(i, "SGGG")
         load_w(0, (all_rows,))
         load_h(0, (all_rows,))
         load_w(1, (all_rows,))
         load_feat(0, (all_rows,))
-        for i in range(1, TOTAL):
+        for i in range(1, SINGLES):
             if new_w(i + 1) is not None:
                 load_w(new_w(i + 1), (all_rows,))
-            if new_h(i + 2) is not None:
-                load_h(new_h(i + 2), (all_rows,))
+            if i == 2:
+                load_h(1, (all_rows,))
             load_feat(i, (all_rows,))
+        for i in range(SINGLES, TOTAL, 2):
+            if i == SINGLES + 2:
+                load_h_pair(2)
+            load_feat_pair(i)
         regroup_h(0)
         transpose_w(0)
         regroup_w(0)
@@ -379,9 +398,9 @@ def tile_crossattention_pa_kernel(tc, feat, h_attn, w_out, b_out, gamma, beta, o
                         projected.add((nxt, jj))
             for b in range(1, BATCH):
                 first = [k for k in range(TOTAL) if new_h(k) == b][0]
-                for half in range(2):
-                    if t == ROWS * first - [11,9][half]:
-                        spread_h(b, half)
+                for part in range(4):
+                    if t == max(ROWS * first - [15,13,11,9][part], 6):
+                        spread_h(b, part)
             if t < ROWS_ALL and j == 0 and new_w(i + 2) is not None:
                 transpose_w(new_w(i + 2))
             for k in range(TOTAL):
@@ -415,5 +434,8 @@ def tile_crossattention_pa_kernel(tc, feat, h_attn, w_out, b_out, gamma, beta, o
                     p = plan(k)
                     for r in range(ROWS):
                         normalise(k, r, {"S": nc.scalar, "G": nc.gpsimd, "V": nc.vector}[p[r]])
-                    store(k, halves[0])
-                    store(k, halves[1])
+                    if k < TOTAL - 1:
+                        store(k, all_rows)
+                    else:
+                        store(k, halves[0])
+                        store(k, halves[1])

@@ -327,8 +327,8 @@ def tile_crossattention_pa_kernel(tc, feat, h_attn, w_out, b_out, gamma, beta, o
             else:
                 engine.tensor_scalar(out=row, in0=row, scalar1=gain_j, scalar2=shift_j, op0=ALU.mult, op1=ALU.add)
 
-        def store(i, rows):
-            nc.sync.dma_start(out=out_v[order[i][0] * SLABS + order[i][1]][:, rows, :], in_=x_sb[i][:, rows, :])
+        def store(i, rows, queue=nc.sync):
+            queue.dma_start(out=out_v[order[i][0] * SLABS + order[i][1]][:, rows, :], in_=x_sb[i][:, rows, :])
 
         ctx.enter_context(tc.manual_schedule())
 
@@ -337,7 +337,7 @@ def tile_crossattention_pa_kernel(tc, feat, h_attn, w_out, b_out, gamma, beta, o
         halves = (half_rows(0), half_rows(1))
         ROWS_ALL = TOTAL * ROWS
         off = lambda i: (4, 5, 7, 8)
-        plan = lambda i: {TOTAL - 3: "SVGG", TOTAL - 2: "SSVV", TOTAL - 1: "SSVV"}.get(i, "SGGG")
+        plan = lambda i: {TOTAL - 3: "SVGG", TOTAL - 2: "SSVV", TOTAL - 1: "SSVV", 0: "GGGG", 4: "GGGG", 8: "GGGG"}.get(i, "SGGG")
         load_w(0, (all_rows,))
         load_h(0, (all_rows,))
         load_w(1, (all_rows,))
@@ -434,8 +434,8 @@ def tile_crossattention_pa_kernel(tc, feat, h_attn, w_out, b_out, gamma, beta, o
                     p = plan(k)
                     for r in range(ROWS):
                         normalise(k, r, {"S": nc.scalar, "G": nc.gpsimd, "V": nc.vector}[p[r]])
-                    if k < TOTAL - 1:
-                        store(k, all_rows)
+                    if k < LAST:
+                        store(k, all_rows, nc.scalar if k == LAST - 2 else nc.sync)
                     else:
-                        store(k, halves[0])
+                        store(k, halves[0], nc.scalar)
                         store(k, halves[1])

from contextlib import ExitStack

import concourse.mybir as mybir
from concourse.masks import make_identity

F32 = mybir.dt.float32
BF16 = mybir.dt.bfloat16
U32 = mybir.dt.uint32
U8 = mybir.dt.uint8
FP8X4 = mybir.dt.float8_e4m3fn_x4
ALU = mybir.AluOpType
ACT = mybir.ActivationFunctionType
AX = mybir.AxisListType

P = 128
PACK = 4
BATCH = 4
CHANNELS = 2048
K = 512
N = 512
GROUP = 128
EPS = 1e-5

ROWS = 4
HALF = ROWS // 2
SLAB = P * ROWS
SLABS = CHANNELS // SLAB
TOTAL = BATCH * SLABS
LAST = TOTAL - 1
QUADRANT = GROUP // ROWS

FLOPS = 2 * BATCH * CHANNELS * K * N

SINGLES = 4
ROWS_ON_SCALAR = 1


def tile_crossattention_pa_kernel(tc, feat, h_attn, w_out, b_out, gamma, beta, out):
    nc = tc.nc

    feat_v = feat.rearrange("b (s p j) h w -> (b s) p j (h w)", p=P, j=ROWS)
    out_v = out.rearrange("b (s p j) h w -> (b s) p j (h w)", p=P, j=ROWS)
    w_v = w_out.rearrange("(s p j) k -> s p j k", p=P, j=ROWS)
    h_v = h_attn.rearrange("b (q t) h w -> b q t (h w)", t=PACK)

    with ExitStack() as ctx:
        const = ctx.enter_context(tc.tile_pool(name="const", bufs=1))
        raw = ctx.enter_context(tc.tile_pool(name="raw", bufs=4))
        grouped = ctx.enter_context(tc.tile_pool(name="grouped", bufs=2))
        feats = ctx.enter_context(tc.tile_pool(name="feats", bufs=SINGLES))
        feat_pairs = ctx.enter_context(tc.tile_pool(name="feat_pairs", bufs=(TOTAL - SINGLES) // 2))
        h_pairs = ctx.enter_context(tc.tile_pool(name="h_pairs", bufs=1))
        xs = ctx.enter_context(tc.tile_pool(name="xs", bufs=9))
        junk = ctx.enter_context(tc.tile_pool(name="junk", bufs=3))
        small = ctx.enter_context(tc.tile_pool(name="small", bufs=4))
        psum_y = ctx.enter_context(tc.psum_pool(name="psum_y", bufs=5))
        psum_const = ctx.enter_context(tc.psum_pool(name="psum_const", bufs=1))
        psum_s = ctx.enter_context(tc.psum_pool(name="psum_s", bufs=2))

        eps = const.tile([P, 1], F32)
        nc.vector.memset(eps[:], EPS)
        warm = const.tile([P, 1], F32)
        nc.scalar.activation(out=warm[:], in_=eps[:], func=ACT.Abs_reciprocal_sqrt)

        ident = const.tile([P, P], F32)
        make_identity(nc, ident[:])
        ident_bf = const.tile([P, P], BF16)
        nc.gpsimd.tensor_copy(out=ident_bf[:], in_=ident[:])

        group_avg = const.tile([P, P], F32)
        nc.vector.memset(group_avg[:], 0.0)
        for g in range(P // QUADRANT):
            rows = slice(g * QUADRANT, (g + 1) * QUADRANT)
            nc.vector.memset(group_avg[rows, rows], -1.0 / (GROUP * N))

        params_bf = const.tile([P, 3, SLABS, ROWS], BF16)
        for which, vec in enumerate((b_out, gamma, beta)):
            nc.scalar.dma_start(
                out=params_bf[:, which], in_=vec.rearrange("(s p j) -> p s j", p=P, j=ROWS)
            )
        params = const.tile([P, 3, SLABS, ROWS], F32)

        w_codes = const.tile([P, SLABS, SLAB], U32, align_bytes=64)
        w_scales = const.tile([P, SLABS, SLAB], U8, align_bytes=64)
        h_codes = const.tile([P, BATCH, N], U32, align_bytes=64)
        h_scales = const.tile([P, BATCH, N], U8, align_bytes=64)

        h_raw = {}
        w_raw = {}
        h_grouped = {}
        h_spread = {}
        w_grouped = {}
        w_transposed = {}
        feat_sb = {}
        y_ps = {}
        x_sb = {}
        sums_sb = {}
        mom_ps = {}
        neg_mean_sb = {}
        neg_var_sb = {}
        rstd_sb = {}
        gain_sb = {}
        shift_sb = {}

        order = []
        for b in range(BATCH):
            order.extend([(b, s) for s in range(SLABS)])

        def new_h(i):
            if i < TOTAL and order[i][1] == 0:
                return order[i][0]
            return None

        def new_w(i):
            if i < TOTAL and order[i][0] == 0:
                return order[i][1]
            return None

        def half_rows(half):
            return slice(half * HALF, (half + 1) * HALF)

        def load_w(s, halves):
            if s not in w_raw:
                w_tile = raw.tile([P, ROWS, K], BF16)
                w_raw[s] = w_tile
            for rows in halves:
                nc.sync.dma_start(out=w_raw[s][:, rows, :], in_=w_v[s][:, rows, :])

        def load_h(b, pieces):
            h_tile = raw.tile([P, PACK, N], BF16)
            for values in pieces:
                nc.sync.dma_start(out=h_tile[:, values, :], in_=h_v[b][:, values, :])
            h_raw[b] = h_tile

        def load_feat_pair(i):
            pair = feat_pairs.tile([P, 2, ROWS, N], BF16)
            nc.sync.dma_start(out=pair[:], in_=feat_v[i : i + 2].rearrange("s p j n -> p s j n"))
            feat_sb[i] = pair[:, 0]
            feat_sb[i + 1] = pair[:, 1]

        def load_h_pair(b):
            pair = h_pairs.tile([P, 2, PACK, N], BF16)
            nc.sync.dma_start(out=pair[:], in_=h_v[b : b + 2].rearrange("b q t n -> q b t n"))
            h_raw[b] = pair[:, 0]
            h_raw[b + 1] = pair[:, 1]

        def load_feat(i, pieces):
            if i not in feat_sb:
                feat_tile = feats.tile([P, ROWS, N], BF16)
                feat_sb[i] = feat_tile
            for rows in pieces:
                nc.sync.dma_start(out=feat_sb[i][:, rows, :], in_=feat_v[order[i][0] * SLABS + order[i][1]][:, rows, :])

        def transpose_w(s):
            w_words = w_raw[s][:].rearrange("p j k -> p (j k)").bitcast(F32)
            for half in range(2):
                bank = psum_y.tile([P, N], F32)
                w_t = bank[:].rearrange("q (jj u p) -> q jj u p", jj=HALF, u=2)
                for jj in range(HALF):
                    for u in range(2):
                        row = (HALF * half + jj) * 2 * P
                        nc.tensor.transpose(w_t[:, jj, u, :], w_words[:, row + u : row + 2 * P : 2], ident[:])
                w_transposed[(s, half)] = w_t

        def regroup_w(s):
            w_group = grouped.tile([P, ROWS * P * PACK], BF16, align_bytes=64)
            w_group_words = w_group[:].bitcast(F32).rearrange("q (j p u) -> q j p u", j=ROWS, u=2)
            for half in range(2):
                nc.scalar.copy(
                    out=w_group_words[:, half_rows(half)],
                    in_=w_transposed[(s, half)].rearrange("q jj u p -> q jj p u"),
                )
            w_grouped[s] = w_group

        def regroup_h(b):
            h_group = grouped.tile([P, N, PACK], BF16, align_bytes=64)
            dst = h_group[:].rearrange("q (c i) t -> q c t i", i=4)
            src = h_raw[b][:].rearrange("q t (c i) -> q c t i", i=4)
            nc.vector.tensor_copy(out=dst, in_=src)
            h_grouped[b] = h_group

        def spread_h(b, part):
            half, side = divmod(part, 2)
            if side == 0:
                bank = psum_y.tile([P, N // 2, PACK], BF16)
                h_spread[(b, half)] = bank
            nc.tensor.matmul(
                out=h_spread[(b, half)][:, side * P : (side + 1) * P, :],
                lhsT=ident_bf[:],
                rhs=h_raw[b][:, :, part * P : (part + 1) * P].rearrange("q t n -> q n t"),
                start=True,
                stop=True,
            )

        def gather_h(b, half):
            cols = slice(half * N // 2, (half + 1) * N // 2)
            if half == 0:
                h_group = grouped.tile([P, N, PACK], BF16, align_bytes=64)
                h_grouped[b] = h_group
            nc.scalar.copy(out=h_grouped[b][:, cols, :], in_=h_spread[(b, half)][:])

        def quantise_w(s, cols):
            nc.vector.quantize_mx(
                out=w_codes[:, s, cols].bitcast(FP8X4),
                scales=w_scales[:, s, cols],
                in_=w_grouped[s][:, cols.start * PACK : cols.stop * PACK],
            )

        def quantise_h(b):
            nc.vector.quantize_mx(
                out=h_codes[:, b, :].bitcast(FP8X4),
                scales=h_scales[:, b, :],
                in_=h_grouped[b][:].rearrange("q n t -> q (n t)"),
            )

        def project(i, j):
            b, s = order[i]
            bank = psum_y.tile([P, N], F32)
            cols = slice(j * P, (j + 1) * P)
            nc.tensor.matmul_mx(
                out=bank[:],
                lhsT=w_codes[:, s, cols].bitcast(FP8X4),
                lhsT_scale=w_scales[:, s, cols],
                rhs=h_codes[:, b, :].bitcast(FP8X4),
                rhs_scale=h_scales[:, b, :],
                start=True,
                stop=True,
            )
            y_ps[(i, j)] = bank

        def piece_rows(i):
            return 1 if i >= TOTAL - 0 else HALF

        def residual(i, j):
            b, s = order[i]
            n_rows = piece_rows(i)
            if j == 0:
                x = xs.tile([P, ROWS, N], F32)
                x_sb[i] = x
                sums = small.tile([P, ROWS // n_rows, n_rows + 1, 8], F32)
                sums_sb[i] = sums
            nc.vector.scalar_tensor_tensor(
                out=x_sb[i][:, j, :],
                in0=y_ps[(i, j)][:],
                scalar=params[:, 0, s, j : j + 1],
                in1=feat_sb[i][:, j, :],
                op0=ALU.add,
                op1=ALU.add,
                accum_out=sums_sb[i][:, j // n_rows, j % n_rows, 0:1],
            )

        def squares(i, piece):
            n_rows = piece_rows(i)
            sq = junk.tile([P, HALF * N], BF16)
            nc.scalar.activation(
                out=sq[:, : n_rows * N],
                in_=x_sb[i][:, piece * n_rows : (piece + 1) * n_rows, :].rearrange("p j n -> p (j n)"),
                func=ACT.Square,
                accum_out=sums_sb[i][:, piece, n_rows, 0:1],
            )

        def moments(i, piece):
            n_rows = piece_rows(i)
            if piece == 0:
                mom = psum_s.tile([P, HALF + 1], F32)
                mom_ps[i] = mom
            nc.tensor.matmul(
                out=mom_ps[i][:, : n_rows + 1],
                lhsT=group_avg[:],
                rhs=sums_sb[i][:, piece, :, 0],
                start=(piece == 0),
                stop=(piece == ROWS // n_rows - 1),
            )

        def mean(i):
            neg_mean = small.tile([P, 1], F32)
            nc.vector.tensor_reduce(out=neg_mean[:], in_=mom_ps[i][:, : piece_rows(i)], axis=AX.X, op=ALU.add)
            neg_mean_sb[i] = neg_mean

        def variance(i):
            neg_var = small.tile([P, 1], F32)
            n_rows = piece_rows(i)
            nc.vector.scalar_tensor_tensor(
                out=neg_var[:],
                in0=neg_mean_sb[i][:],
                scalar=neg_mean_sb[i][:, 0:1],
                in1=mom_ps[i][:, n_rows : n_rows + 1],
                op0=ALU.mult,
                op1=ALU.add,
            )
            neg_var_sb[i] = neg_var

        def inv_std(i):
            rstd = small.tile([P, 1], F32)
            nc.scalar.activation(
                out=rstd[:], in_=neg_var_sb[i][:], func=ACT.Abs_reciprocal_sqrt, bias=eps[:, 0:1], scale=-1.0
            )
            rstd_sb[i] = rstd

        def make_gain(i):
            b, s = order[i]
            gain = small.tile([P, ROWS], F32)
            nc.vector.tensor_scalar(
                out=gain[:], in0=affine_ps[:, 0, s, :], scalar1=rstd_sb[i][:, 0:1], scalar2=None, op0=ALU.mult
            )
            gain_sb[i] = gain

        def make_shift(i):
            b, s = order[i]
            shift = small.tile([P, ROWS], F32)
            nc.vector.scalar_tensor_tensor(
                out=shift[:],
                in0=gain_sb[i][:],
                scalar=neg_mean_sb[i][:, 0:1],
                in1=affine_ps[:, 1, s, :],
                op0=ALU.mult,
                op1=ALU.add,
            )
            shift_sb[i] = shift

        def normalise(i, j, engine):
            row = x_sb[i][:, j, :]
            gain_j = gain_sb[i][:, j : j + 1]
            shift_j = shift_sb[i][:, j : j + 1]
            if engine is nc.scalar:
                nc.scalar.activation(out=row, in_=row, func=ACT.Identity, bias=shift_j, scale=gain_j)
            else:
                engine.tensor_scalar(out=row, in0=row, scalar1=gain_j, scalar2=shift_j, op0=ALU.mult, op1=ALU.add)

        def store(i, rows, queue=nc.sync):
            queue.dma_start(out=out_v[order[i][0] * SLABS + order[i][1]][:, rows, :], in_=x_sb[i][:, rows, :])

        ctx.enter_context(tc.manual_schedule())

        all_rows = slice(0, ROWS)
        all_cols = slice(0, SLAB)
        halves = (half_rows(0), half_rows(1))
        ROWS_ALL = TOTAL * ROWS
        off = lambda i: (4, 5, 7, 8)
        plan = lambda i: {TOTAL - 3: "SVGG", TOTAL - 2: "SSVV", TOTAL - 1: "SSVV", 0: "GGGG", 4: "GGGG", 8: "GGGG"}.get(i, "SGGG")
        load_w(0, (all_rows,))
        load_h(0, (all_rows,))
        load_w(1, (all_rows,))
        load_feat(0, (all_rows,))
        for i in range(1, SINGLES):
            if new_w(i + 1) is not None:
                load_w(new_w(i + 1), (all_rows,))
            if i == 2:
                load_h(1, (all_rows,))
            load_feat(i, (all_rows,))
        for i in range(SINGLES, TOTAL, 2):
            if i == SINGLES + 2:
                load_h_pair(2)
            load_feat_pair(i)
        regroup_h(0)
        transpose_w(0)
        regroup_w(0)
        transpose_w(1)
        regroup_w(1)
        quantise_w(0, slice(0, SLAB // 2))
        quantise_h(0)
        quantise_w(0, slice(SLAB // 2, SLAB))
        nc.vector.tensor_copy(out=params[:], in_=params_bf[:])
        for j in range(ROWS):
            project(0, j)
        affine_ps = psum_const.tile([P, 2, SLABS, ROWS], F32)
        nc.tensor.matmul(
            out=affine_ps[:].rearrange("p a s j -> p (a s j)"),
            lhsT=ident[:],
            rhs=params[:, 1:3].rearrange("p a s j -> p (a s j)"),
            start=True,
            stop=True,
        )

        projected = set((0, j) for j in range(ROWS))
        for t in range(ROWS_ALL + 12):
            i, j = divmod(t, ROWS)
            nxt = i + 1
            if t < ROWS_ALL and j == 0 and False:
                if new_w(nxt) is not None:
                    quantise_w(new_w(nxt), all_cols)
                if new_h(nxt) is not None:
                    quantise_h(new_h(nxt))
            if t < ROWS_ALL:
                residual(i, j)
            if t < ROWS_ALL and nxt < TOTAL:
                fresh = new_w(nxt) is not None or new_h(nxt) is not None
                if j == 9 and new_h(i + 1) is not None:
                    regroup_h(new_h(i + 1))
                if j == 1:
                    if new_w(nxt) is not None:
                        quantise_w(new_w(nxt), all_cols)
                    if new_h(nxt) is not None:
                        quantise_h(new_h(nxt))
                for jj in range(j + 1):
                    if (nxt, jj) not in projected and (not fresh or j >= 1):
                        project(nxt, jj)
                        projected.add((nxt, jj))
            for b in range(1, BATCH):
                first = [k for k in range(TOTAL) if new_h(k) == b][0]
                for part in range(4):
                    if t == max(ROWS * first - [15,13,11,9][part], 6):
                        spread_h(b, part)
            if t < ROWS_ALL and j == 0 and new_w(i + 2) is not None:
                transpose_w(new_w(i + 2))
            for k in range(TOTAL):
                last = ROWS * k + ROWS - 1
                m, v, g, h = off(k)
                if t == last + m:
                    mean(k)
                if t == last + v:
                    variance(k)
                if t == last + g:
                    make_gain(k)
                if t == last + h:
                    make_shift(k)
            if t < ROWS_ALL:
                n_rows = piece_rows(i)
                if j % n_rows == n_rows - 1:
                    squares(i, j // n_rows)
                    if j == 1 and new_w(i + 2) is not None:
                        regroup_w(new_w(i + 2))
                    moments(i, j // n_rows)
            for b in range(1, BATCH):
                first = [k for k in range(TOTAL) if new_h(k) == b][0]
                for half in range(2):
                    if t == ROWS * first - [7,6][half]:
                        gather_h(b, half)
            for k in range(TOTAL):
                if t == ROWS * k + ROWS - 1 + off(k)[1]:
                    inv_std(k)
            for k in range(TOTAL):
                if t == ROWS * k + ROWS - 1 + off(k)[3]:
                    p = plan(k)
                    for r in range(ROWS):
                        normalise(k, r, {"S": nc.scalar, "G": nc.gpsimd, "V": nc.vector}[p[r]])
                    if k < LAST:
                        store(k, all_rows, nc.scalar if k == LAST - 2 else nc.sync)
                    else:
                        store(k, halves[0], nc.scalar)
                        store(k, halves[1])
